import numpy as np
import ml_dtypes


def mxq(x, axis, fmt="e4m3"):
    dtype, down = {"e4m3": (ml_dtypes.float8_e4m3fn, 7), "e5m2": (ml_dtypes.float8_e5m2, 14)}[fmt]
    v = np.moveaxis(np.asarray(x, np.float32).astype(ml_dtypes.bfloat16).astype(np.float64), axis, -1)
    blocks = v.reshape(v.shape[:-1] + (-1, 32))
    amax = np.abs(blocks).max(-1, keepdims=True)
    byte = np.maximum(np.where(amax > 0, np.frexp(amax)[1] - 1 + 127, 0) - down, 1)
    scale = np.exp2(byte - 127.0)
    codes = (blocks / scale).astype(np.float32).astype(dtype).astype(np.float64)
    return np.moveaxis((codes * scale).reshape(v.shape), -1, axis)


WIDE = False


def mx_kscale(k):
    if not WIDE:
        return np.ones(k)
    levels = np.array([10, -10, 5, -5, 0])
    if k % 512:
        return np.exp2(np.random.permutation(np.resize(levels, k // 32))).repeat(32)
    a = np.empty((k // 512, 16))
    for p in range(k // 512):
        a[p, :8] = np.random.permutation(np.resize(levels, 8))
        for g in range(8):
            far = levels[np.abs(levels - a[p, g]) >= 10]
            a[p, g + 8] = far[np.random.randint(len(far))]
    return np.exp2(a.ravel()).repeat(32)


BF16 = ml_dtypes.bfloat16


def bf(x):
    return np.asarray(x, np.float32).astype(BF16)


def f64(x):
    return np.asarray(x).astype(np.float64)


B, G, C, F, NC = 128, 6, 1024, 1024, 4096
HW = G * G
P_GEM = 3.0
EPS_GEM = 1e-6
EPS_NORM = 1e-12


def l2n(v, axis):
    n = np.sqrt(np.sum(v * v, axis=axis, keepdims=True))
    return v / np.maximum(n, EPS_NORM)


def setup_inputs():
    s, t = mx_kscale(F), mx_kscale(C)
    z = np.random.standard_normal((B, HW, F))
    return {"hdn": bf(z / (1.0 + np.exp(-1.702 * z)) * s),
            "fc2_w": bf(np.random.standard_normal((F, C)) * 1.5 / np.sqrt(F) / s[:, None] * t),
            "fc2_b": bf(np.random.standard_normal(C) * 0.3 * t),
            "head_w": bf(np.random.standard_normal((C, NC)) / np.sqrt(C) / t[:, None]),
            "head_b": bf(np.random.standard_normal(NC) * 0.3)}


def reference(hdn, fc2_w, fc2_b, head_w, head_b):
    tok = (mxq(f64(hdn), 2, "e4m3") @ mxq(f64(fc2_w), 0, "e4m3")) + f64(fc2_b)
    g = np.mean(np.maximum(tok, EPS_GEM) ** P_GEM, axis=1) ** (1.0 / P_GEM)
    desc = (mxq(g, 1, "e4m3") @ mxq(f64(head_w), 0, "e4m3")) + f64(head_b)
    return l2n(desc, 1)

@@ -1,0 +1,381 @@
+from contextlib import ExitStack
+
+import concourse.mybir as mybir
+from concourse.masks import make_identity
+
+F32 = mybir.dt.float32
+BF16 = mybir.dt.bfloat16
+U32 = mybir.dt.uint32
+U8 = mybir.dt.uint8
+FP8X4 = mybir.dt.float8_e4m3fn_x4
+ALU = mybir.AluOpType
+ACT = mybir.ActivationFunctionType
+AX = mybir.AxisListType
+
+P = 128
+NB = 128
+NT = 36
+NF = 1024
+NCH = 1024
+NOUT = 4096
+EPS3 = 1e-18
+BIG = 3.0e38
+NSTEP = 18
+NPART = 18
+V_COLS = 240
+S_MID = 376
+
+FLOPS = 2 * NB * NT * NF * NCH + 2 * NB * NCH * NOUT
+
+
+def tile_tokenmudule_pb_kernel(tc, hdn, fc2_w, fc2_b, head_w, head_b, out):
+    nc = tc.nc
+    with ExitStack() as ctx:
+        const = ctx.enter_context(tc.tile_pool(name="const", bufs=1))
+        hr_pool = ctx.enter_context(tc.tile_pool(name="hr", bufs=3))
+        hg_pool = ctx.enter_context(tc.tile_pool(name="hg", bufs=2))
+        hc_pool = ctx.enter_context(tc.tile_pool(name="hc", bufs=3))
+        raw_pool = ctx.enter_context(tc.tile_pool(name="raw", bufs=3))
+        grp_pool = ctx.enter_context(tc.tile_pool(name="grp", bufs=2))
+        s_pool = ctx.enter_context(tc.tile_pool(name="sq", bufs=2))
+        c_pool = ctx.enter_context(tc.tile_pool(name="cube", bufs=3))
+        ps_sum = ctx.enter_context(tc.psum_pool(name="pssum", bufs=1))
+        ps_mm = ctx.enter_context(tc.psum_pool(name="psmm", bufs=4))
+        ps_xt = ctx.enter_context(tc.psum_pool(name="psxt", bufs=2))
+        ctx.enter_context(tc.manual_schedule())
+
+        ident_f = const.tile([P, P], F32)
+        ident_b = const.tile([P, P], BF16)
+        brow = const.tile([P, P], BF16)
+        bias = const.tile([P, 8], F32)
+        one = const.tile([P, 1], F32)
+        dmy = const.tile([P, 1], F32)
+        w_codes = const.tile([P, 2, 2, 512], U32, align_bytes=64)
+        w_scales = const.tile([P, 2, 2, 512], U8, align_bytes=64)
+        hw_codes = const.tile([P, 8, 2, 512], U32, align_bytes=64)
+        hw_scales = const.tile([P, 8, 2, 512], U8, align_bytes=64)
+        hb = const.tile([P, NOUT], BF16)
+        d = const.tile([P, NOUT], F32)
+        junk = const.tile([P, 512], F32)
+        lng = const.tile([P, NCH], F32)
+        g_grp = const.tile([P, 2, P, 4], BF16, align_bytes=64)
+        g_codes = const.tile([P, 2, P], U32, align_bytes=64)
+        g_scales = const.tile([P, 2, P], U8, align_bytes=64)
+        ss = const.tile([P, 8], F32)
+        tot = const.tile([P, 1], F32)
+        nrm = const.tile([P, 1], F32)
+        rinv = const.tile([P, 1], F32)
+        sums = [ps_sum.tile([P, 512], F32, name="sum%d" % i) for i in range(2)]
+
+        hr = {}
+        hg = {}
+        hc = {}
+        hs = {}
+        raw = {}
+        grp = {}
+        xts = {}
+        banks = {}
+        s4 = {}
+        c4 = {}
+
+        def load_h(n):
+            hr[n] = hr_pool.tile([P, 4, NF], BF16, name="hr")
+            nc.sync.dma_start(out=hr[n][:], in_=hdn[:, 4 * n : 4 * n + 4, :])
+
+        def load_chunk(ci):
+            raw[ci] = raw_pool.tile([P, 8, 512], BF16, name="raw")
+            if ci < 2:
+                src = fc2_w[:, 512 * ci : 512 * ci + 512]
+            else:
+                src = head_w[:, 512 * (ci - 2) : 512 * (ci - 2) + 512]
+            for g in range(2):
+                nc.sync.dma_start(
+                    out=raw[ci][:, 4 * g : 4 * g + 4, :],
+                    in_=src[512 * g : 512 * g + 512, :].rearrange("(p t) c -> p t c", t=4),
+                )
+
+        def regroup(eng_copy, r, n0, n1):
+            ci, g = divmod(r, 2)
+            src = raw[ci][:, 4 * g : 4 * g + 4, n0:n1]
+            dst = grp[ci][:, g, n0:n1, :]
+            eng_copy(
+                out=dst.rearrange("p (c i) t -> p c t i", i=4),
+                in_=src.rearrange("p t (c i) -> p c t i", i=4),
+            )
+
+        def rg_v(r):
+            ci, g = divmod(r, 2)
+            if g == 0:
+                grp[ci] = grp_pool.tile([P, 2, 512, 4], BF16, name="grp", align_bytes=64)
+            regroup(nc.vector.tensor_copy, r, 0, V_COLS)
+
+        def rg_s(r, piece):
+            if piece == 0:
+                regroup(nc.scalar.copy, r, V_COLS, S_MID)
+            else:
+                regroup(nc.scalar.copy, r, S_MID, 512)
+
+        def cq(r):
+            ci, g = divmod(r, 2)
+            if ci < 2:
+                codes, scales = w_codes[:, ci, g, :], w_scales[:, ci, g, :]
+            else:
+                codes, scales = hw_codes[:, ci - 2, g, :], hw_scales[:, ci - 2, g, :]
+            nc.vector.quantize_mx(
+                out=codes.bitcast(FP8X4),
+                scales=scales,
+                in_=grp[ci][:, g, :, :].rearrange("p n j -> p (n j)"),
+            )
+
+        def hdn_t(q, tp):
+            n, g = divmod(q, 2)
+            xt = ps_xt.tile([P, 2, 256], F32, name="xt")
+            for u in range(2):
+                for t2 in range(2):
+                    nc.tensor.transpose(
+                        out=xt[:, u, P * t2 : P * t2 + P],
+                        in_=hr[n][:, 2 * tp + t2, :].bitcast(F32)[:, 256 * g + u : 256 * g + 256 : 2],
+                        identity=ident_f[:],
+                    )
+            xts[(q, tp)] = xt
+
+        def t_out(q, tp):
+            n, g = divmod(q, 2)
+            if g == 0 and tp == 0:
+                hg[n] = hg_pool.tile([P, 2, 2048], BF16, name="hg", align_bytes=64)
+            g32 = hg[n][:, g, :].bitcast(F32)
+            nc.scalar.copy(
+                out=g32[:, 512 * tp : 512 * tp + 512].rearrange("p (c u) -> p c u", u=2),
+                in_=xts[(q, tp)][:].rearrange("p u c -> p c u"),
+            )
+
+        def hq(q):
+            n, g = divmod(q, 2)
+            if g == 0:
+                hc[n] = hc_pool.tile([P, 2, 512], U32, name="hc", align_bytes=64)
+                hs[n] = hc_pool.tile([P, 2, 512], U8, name="hs", align_bytes=64)
+            nc.vector.quantize_mx(out=hc[n][:, g, :].bitcast(FP8X4), scales=hs[n][:, g, :], in_=hg[n][:, g, :])
+
+        def mx(k, mms):
+            n, h = divmod(k, 2)
+            for mm in mms:
+                ps = ps_mm.tile([P, 512], F32, name="mm")
+                for g in range(2):
+                    nc.tensor.matmul_mx(
+                        out=ps[:],
+                        lhsT=w_codes[:, h, g, P * mm : P * mm + P].bitcast(FP8X4),
+                        lhsT_scale=w_scales[:, h, g, P * mm : P * mm + P],
+                        rhs=hc[n][:, g, :].bitcast(FP8X4),
+                        rhs_scale=hs[n][:, g, :],
+                        start=(g == 0),
+                        stop=(g == 1),
+                    )
+                banks[(k, mm)] = ps
+
+        def sq(k, mm):
+            m = 4 * (k % 2) + mm
+            if mm == 0:
+                s4[k] = s_pool.tile([P, 4, 512], F32, name="s4")
+            nc.scalar.activation(
+                out=s4[k][:, mm, :], in_=banks[(k, mm)][:], func=ACT.Square, bias=bias[:, m : m + 1], scale=1.0
+            )
+
+        def stt(k, mm):
+            m = 4 * (k % 2) + mm
+            if mm == 0:
+                c4[k] = c_pool.tile([P, 4, 512], F32, name="c4")
+            nc.vector.scalar_tensor_tensor(
+                out=c4[k][:, mm, :],
+                in0=banks[(k, mm)][:],
+                scalar=bias[:, m : m + 1],
+                in1=s4[k][:, mm, :],
+                op0=ALU.add,
+                op1=ALU.mult,
+            )
+
+        def clamp_g(k, mm):
+            nc.gpsimd.tensor_scalar(
+                out=c4[k][:, mm, :], in0=c4[k][:, mm, :], scalar1=BIG, scalar2=EPS3, op0=ALU.min, op1=ALU.max
+            )
+
+        def clamp_v(k):
+            both = c4[k][:, 2:4, :].rearrange("p m c -> p (m c)")
+            nc.vector.tensor_scalar_max(out=both, in0=both, scalar1=EPS3)
+
+        def sum_t(k, mms):
+            n, h = divmod(k, 2)
+            for mm in mms:
+                for ts in range(4):
+                    nc.tensor.matmul(
+                        out=sums[h][:, P * mm : P * mm + P],
+                        lhsT=c4[k][:, mm, P * ts : P * ts + P],
+                        rhs=ident_f[:],
+                        is_transpose=True,
+                        start=(n == 0 and mm == 0 and ts == 0),
+                        stop=(n == 8 and mm == 3 and ts == 3),
+                    )
+
+        make_identity(nc, ident_f[:])
+        make_identity(nc, ident_b[:])
+        nc.vector.memset(brow[:], 0.0)
+        nc.vector.memset(one[:], 1.0)
+        nc.scalar.dma_start(out=brow[0:8, :], in_=fc2_b.rearrange("(m p) -> m p", p=P))
+        load_h(0)
+        load_chunk(0)
+        load_chunk(1)
+        load_h(1)
+        load_h(2)
+        load_chunk(2)
+
+        bt = ps_xt.tile([P, P], BF16, name="xt")
+        nc.tensor.transpose(out=bt[:], in_=brow[:], identity=ident_b[:])
+        nc.vector.tensor_copy(out=bias[:], in_=bt[:, 0:8])
+
+        for q in range(2):
+            for tp in range(2):
+                hdn_t(q, tp)
+            for tp in range(2):
+                t_out(q, tp)
+        load_h(3)
+        hq(0)
+        hq(1)
+        for r in range(2):
+            rg_v(r)
+            rg_s(r, 0)
+            rg_s(r, 1)
+        cq(0)
+        cq(1)
+
+        for k in range(NSTEP):
+            chunk_work = k >= 1 and 4 <= k + 3 <= 19
+            mx(k, [0, 1])
+            if k >= 2:
+                sum_t(k - 2, [2, 3])
+            if k == 0:
+                hdn_t(2, 0)
+                hdn_t(2, 1)
+                for r in range(2, 4):
+                    rg_v(r)
+                    rg_s(r, 0)
+                    rg_s(r, 1)
+                load_chunk(3)
+                load_chunk(4)
+            else:
+                if k + 3 < NPART:
+                    hdn_t(k + 3, 0)
+                if k + 2 < NPART:
+                    t_out(k + 2, 1)
+            sq(k, 0)
+            sq(k, 1)
+            if k == 0:
+                t_out(2, 0)
+                t_out(2, 1)
+                cq(2)
+                cq(3)
+            else:
+                clamp_v(k - 1)
+            if k + 2 < NPART:
+                hq(k + 2)
+            if k >= 1 and 4 <= k + 2 <= 19:
+                cq(k + 2)
+            if chunk_work:
+                rg_v(k + 3)
+                rg_s(k + 3, 0)
+            mx(k, [2, 3])
+            if k >= 1:
+                sum_t(k - 1, [0, 1])
+            if k == 0:
+                hdn_t(3, 0)
+            elif k + 3 < NPART:
+                hdn_t(k + 3, 1)
+            if k + 3 < NPART:
+                t_out(k + 3, 0)
+            if k == 0:
+                hdn_t(3, 1)
+            sq(k, 2)
+            sq(k, 3)
+            if chunk_work:
+                rg_s(k + 3, 1)
+            for mm in range(4):
+                stt(k, mm)
+                if mm < 2:
+                    clamp_g(k, mm)
+            if k % 2 == 0:
+                if k // 2 + 4 <= 8:
+                    load_h(k // 2 + 4)
+                if k >= 2 and k // 2 + 4 <= 9:
+                    load_chunk(k // 2 + 4)
+            if k == 12:
+                nc.sync.dma_start(out=hb[:], in_=head_b.partition_broadcast(P))
+
+        def ln_half(h):
+            nc.scalar.activation(
+                out=lng[:, 512 * h : 512 * h + 512].rearrange("b (t p) -> b t p", t=4),
+                in_=sums[h][:].rearrange("b (p t) -> b t p", t=4),
+                func=ACT.Ln,
+                scale=1.0 / NT,
+            )
+
+        clamp_v(NSTEP - 1)
+        sum_t(NSTEP - 2, [2, 3])
+        ln_half(0)
+        sum_t(NSTEP - 1, [0, 1])
+        sum_t(NSTEP - 1, [2, 3])
+        ln_half(1)
+
+        ps2 = {}
+
+        def head_pass(nt, g):
+            nc.tensor.matmul_mx(
+                out=ps2[nt][:],
+                lhsT=g_codes[:, g, :].bitcast(FP8X4),
+                lhsT_scale=g_scales[:, g, :],
+                rhs=hw_codes[:, nt, g, :].bitcast(FP8X4),
+                rhs_scale=hw_scales[:, nt, g, :],
+                start=(g == 0),
+                stop=(g == 1),
+            )
+
+        lts = []
+        for g in range(2):
+            lt = ps_xt.tile([P, 4, P], F32, name="xt")
+            for j in range(4):
+                a = 4 * g + j
+                nc.tensor.transpose(out=lt[:, j, :], in_=lng[:, P * a : P * a + P], identity=ident_f[:])
+            lts.append(lt)
+        for g in range(2):
+            nc.scalar.activation(
+                out=g_grp[:, g, :, :], in_=lts[g][:].rearrange("p j b -> p b j"), func=ACT.Exp, scale=1.0 / 3.0
+            )
+            nc.vector.quantize_mx(
+                out=g_codes[:, g, :].bitcast(FP8X4),
+                scales=g_scales[:, g, :],
+                in_=g_grp[:, g, :, :].rearrange("p b j -> p (b j)"),
+            )
+            if g == 0:
+                for nt in range(6):
+                    if nt < 4:
+                        ps2[nt] = ps_mm.tile([P, 512], F32, name="mm")
+                    else:
+                        ps2[nt] = ps_sum.tile([P, 512], F32, name="sum%d" % (nt - 4))
+                    head_pass(nt, 0)
+        nc.scalar.activation(out=dmy[:], in_=one[:], func=ACT.Abs_reciprocal_sqrt)
+        for nt in range(8):
+            if nt >= 6:
+                ps2[nt] = ps_xt.tile([P, 512], F32, name="xt")
+                head_pass(nt, 0)
+            head_pass(nt, 1)
+        for nt in range(8):
+            cols = slice(512 * nt, 512 * nt + 512)
+            nc.vector.tensor_tensor(out=d[:, cols], in0=ps2[nt][:], in1=hb[:, cols], op=ALU.add)
+            nc.scalar.activation(out=junk[:], in_=d[:, cols], func=ACT.Square, accum_out=ss[:, nt : nt + 1])
+        nc.scalar.activation(out=junk[:, 0:8], in_=ss[:], func=ACT.Identity, accum_out=tot[:])
+        nc.scalar.activation(out=nrm[:], in_=tot[:], func=ACT.Abs_reciprocal_sqrt)
+        nc.vector.tensor_scalar_min(out=rinv[:], in0=nrm[:], scalar1=1e12)
+        for nt in range(8):
+            cols = slice(512 * nt, 512 * nt + 512)
+            if nt % 3 == 1:
+                nc.scalar.activation(out=d[:, cols], in_=d[:, cols], func=ACT.Copy, scale=rinv[:, 0:1])
+            else:
+                nc.vector.tensor_scalar_mul(out=d[:, cols], in0=d[:, cols], scalar1=rinv[:, 0:1])
+            nc.sync.dma_start(out=out[:, cols], in_=d[:, cols])

@@ -10,7 +10,6 @@ U8 = mybir.dt.uint8
 FP8X4 = mybir.dt.float8_e4m3fn_x4
 ALU = mybir.AluOpType
 ACT = mybir.ActivationFunctionType
-AX = mybir.AxisListType
 
 P = 128
 NB = 128
@@ -20,10 +19,15 @@ NCH = 1024
 NOUT = 4096
 EPS3 = 1e-18
 BIG = 3.0e38
-NSTEP = 18
-NPART = 18
-V_COLS = 240
-S_MID = 376
+V_COLS = 288
+G_TILES = 3
+
+ORDER = (
+    [(0, 0), (1, 0), (0, 1), (1, 1)]
+    + [(n, h) for n in range(2, 7) for h in range(2)]
+    + [(7, 0), (8, 0), (7, 1), (8, 1)]
+)
+NSTEP = len(ORDER)
 
 FLOPS = 2 * NB * NT * NF * NCH + 2 * NB * NCH * NOUT
 
@@ -39,9 +43,7 @@ def tile_tokenmudule_pb_kernel(tc, hdn, fc2_w, fc2_b, head_w, head_b, out):
         grp_pool = ctx.enter_context(tc.tile_pool(name="grp", bufs=2))
         s_pool = ctx.enter_context(tc.tile_pool(name="sq", bufs=2))
         c_pool = ctx.enter_context(tc.tile_pool(name="cube", bufs=3))
-        ps_sum = ctx.enter_context(tc.psum_pool(name="pssum", bufs=1))
-        ps_mm = ctx.enter_context(tc.psum_pool(name="psmm", bufs=4))
-        ps_xt = ctx.enter_context(tc.psum_pool(name="psxt", bufs=2))
+        psum = ctx.enter_context(tc.psum_pool(name="psum", bufs=1))
         ctx.enter_context(tc.manual_schedule())
 
         ident_f = const.tile([P, P], F32)
@@ -65,7 +67,9 @@ def tile_tokenmudule_pb_kernel(tc, hdn, fc2_w, fc2_b, head_w, head_b, out):
         tot = const.tile([P, 1], F32)
         nrm = const.tile([P, 1], F32)
         rinv = const.tile([P, 1], F32)
-        sums = [ps_sum.tile([P, 512], F32, name="sum%d" % i) for i in range(2)]
+
+        def bank(i):
+            return psum.tile([P, 512], F32, name="bank%d" % i)
 
         hr = {}
         hg = {}
@@ -74,13 +78,18 @@ def tile_tokenmudule_pb_kernel(tc, hdn, fc2_w, fc2_b, head_w, head_b, out):
         raw = {}
         grp = {}
         xts = {}
-        banks = {}
+        mm_ps = {}
+        sums = {}
         s4 = {}
         c4 = {}
 
-        def load_h(n):
+        def load_h(n, parts=1):
             hr[n] = hr_pool.tile([P, 4, NF], BF16, name="hr")
-            nc.sync.dma_start(out=hr[n][:], in_=hdn[:, 4 * n : 4 * n + 4, :])
+            w = 4 // parts
+            for i in range(parts):
+                nc.sync.dma_start(
+                    out=hr[n][:, w * i : w * i + w, :], in_=hdn[:, 4 * n + w * i : 4 * n + w * i + w, :]
+                )
 
         def load_chunk(ci):
             raw[ci] = raw_pool.tile([P, 8, 512], BF16, name="raw")
@@ -109,11 +118,8 @@ def tile_tokenmudule_pb_kernel(tc, hdn, fc2_w, fc2_b, head_w, head_b, out):
                 grp[ci] = grp_pool.tile([P, 2, 512, 4], BF16, name="grp", align_bytes=64)
             regroup(nc.vector.tensor_copy, r, 0, V_COLS)
 
-        def rg_s(r, piece):
-            if piece == 0:
-                regroup(nc.scalar.copy, r, V_COLS, S_MID)
-            else:
-                regroup(nc.scalar.copy, r, S_MID, 512)
+        def rg_s(r):
+            regroup(nc.scalar.copy, r, V_COLS, 512)
 
         def cq(r):
             ci, g = divmod(r, 2)
@@ -127,13 +133,13 @@ def tile_tokenmudule_pb_kernel(tc, hdn, fc2_w, fc2_b, head_w, head_b, out):
                 in_=grp[ci][:, g, :, :].rearrange("p n j -> p (n j)"),
             )
 
-        def hdn_t(q, tp):
+        def hdn_t(q, tp, b):
             n, g = divmod(q, 2)
-            xt = ps_xt.tile([P, 2, 256], F32, name="xt")
+            xt = bank(b)
             for u in range(2):
                 for t2 in range(2):
                     nc.tensor.transpose(
-                        out=xt[:, u, P * t2 : P * t2 + P],
+                        out=xt[:, 256 * u + P * t2 : 256 * u + P * t2 + P],
                         in_=hr[n][:, 2 * tp + t2, :].bitcast(F32)[:, 256 * g + u : 256 * g + 256 : 2],
                         identity=ident_f[:],
                     )
@@ -141,12 +147,12 @@ def tile_tokenmudule_pb_kernel(tc, hdn, fc2_w, fc2_b, head_w, head_b, out):
 
         def t_out(q, tp):
             n, g = divmod(q, 2)
-            if g == 0 and tp == 0:
+            if n not in hg:
                 hg[n] = hg_pool.tile([P, 2, 2048], BF16, name="hg", align_bytes=64)
             g32 = hg[n][:, g, :].bitcast(F32)
             nc.scalar.copy(
                 out=g32[:, 512 * tp : 512 * tp + 512].rearrange("p (c u) -> p c u", u=2),
-                in_=xts[(q, tp)][:].rearrange("p u c -> p c u"),
+                in_=xts[(q, tp)][:].rearrange("p (u c) -> p c u", u=2),
             )
 
         def hq(q):
@@ -156,10 +162,10 @@ def tile_tokenmudule_pb_kernel(tc, hdn, fc2_w, fc2_b, head_w, head_b, out):
                 hs[n] = hc_pool.tile([P, 2, 512], U8, name="hs", align_bytes=64)
             nc.vector.quantize_mx(out=hc[n][:, g, :].bitcast(FP8X4), scales=hs[n][:, g, :], in_=hg[n][:, g, :])
 
-        def mx(k, mms):
-            n, h = divmod(k, 2)
-            for mm in mms:
-                ps = ps_mm.tile([P, 512], F32, name="mm")
+        def mx(k):
+            n, h = ORDER[k]
+            for mm in range(4):
+                ps = bank(mm)
                 for g in range(2):
                     nc.tensor.matmul_mx(
                         out=ps[:],
@@ -170,23 +176,23 @@ def tile_tokenmudule_pb_kernel(tc, hdn, fc2_w, fc2_b, head_w, head_b, out):
                         start=(g == 0),
                         stop=(g == 1),
                     )
-                banks[(k, mm)] = ps
+                mm_ps[(k, mm)] = ps
 
         def sq(k, mm):
-            m = 4 * (k % 2) + mm
+            m = 4 * ORDER[k][1] + mm
             if mm == 0:
                 s4[k] = s_pool.tile([P, 4, 512], F32, name="s4")
             nc.scalar.activation(
-                out=s4[k][:, mm, :], in_=banks[(k, mm)][:], func=ACT.Square, bias=bias[:, m : m + 1], scale=1.0
+                out=s4[k][:, mm, :], in_=mm_ps[(k, mm)][:], func=ACT.Square, bias=bias[:, m : m + 1], scale=1.0
             )
 
         def stt(k, mm):
-            m = 4 * (k % 2) + mm
+            m = 4 * ORDER[k][1] + mm
             if mm == 0:
                 c4[k] = c_pool.tile([P, 4, 512], F32, name="c4")
             nc.vector.scalar_tensor_tensor(
                 out=c4[k][:, mm, :],
-                in0=banks[(k, mm)][:],
+                in0=mm_ps[(k, mm)][:],
                 scalar=bias[:, m : m + 1],
                 in1=s4[k][:, mm, :],
                 op0=ALU.add,
@@ -198,13 +204,14 @@ def tile_tokenmudule_pb_kernel(tc, hdn, fc2_w, fc2_b, head_w, head_b, out):
                 out=c4[k][:, mm, :], in0=c4[k][:, mm, :], scalar1=BIG, scalar2=EPS3, op0=ALU.min, op1=ALU.max
             )
 
-        def clamp_v(k):
-            both = c4[k][:, 2:4, :].rearrange("p m c -> p (m c)")
-            nc.vector.tensor_scalar_max(out=both, in0=both, scalar1=EPS3)
+        def clamp_v(k, mm):
+            nc.vector.tensor_scalar_max(out=c4[k][:, mm, :], in0=c4[k][:, mm, :], scalar1=EPS3)
 
-        def sum_t(k, mms):
-            n, h = divmod(k, 2)
-            for mm in mms:
+        def sum_t(k):
+            n, h = ORDER[k]
+            if n == 0:
+                sums[h] = bank(6 + h)
+            for mm in range(4):
                 for ts in range(4):
                     nc.tensor.matmul(
                         out=sums[h][:, P * mm : P * mm + P],
@@ -215,99 +222,6 @@ def tile_tokenmudule_pb_kernel(tc, hdn, fc2_w, fc2_b, head_w, head_b, out):
                         stop=(n == 8 and mm == 3 and ts == 3),
                     )
 
-        make_identity(nc, ident_f[:])
-        make_identity(nc, ident_b[:])
-        nc.vector.memset(brow[:], 0.0)
-        nc.vector.memset(one[:], 1.0)
-        nc.scalar.dma_start(out=brow[0:8, :], in_=fc2_b.rearrange("(m p) -> m p", p=P))
-        load_h(0)
-        load_chunk(0)
-        load_chunk(1)
-        load_h(1)
-        load_h(2)
-        load_chunk(2)
-
-        bt = ps_xt.tile([P, P], BF16, name="xt")
-        nc.tensor.transpose(out=bt[:], in_=brow[:], identity=ident_b[:])
-        nc.vector.tensor_copy(out=bias[:], in_=bt[:, 0:8])
-
-        for q in range(2):
-            for tp in range(2):
-                hdn_t(q, tp)
-            for tp in range(2):
-                t_out(q, tp)
-        load_h(3)
-        hq(0)
-        hq(1)
-        for r in range(2):
-            rg_v(r)
-            rg_s(r, 0)
-            rg_s(r, 1)
-        cq(0)
-        cq(1)
-
-        for k in range(NSTEP):
-            chunk_work = k >= 1 and 4 <= k + 3 <= 19
-            mx(k, [0, 1])
-            if k >= 2:
-                sum_t(k - 2, [2, 3])
-            if k == 0:
-                hdn_t(2, 0)
-                hdn_t(2, 1)
-                for r in range(2, 4):
-                    rg_v(r)
-                    rg_s(r, 0)
-                    rg_s(r, 1)
-                load_chunk(3)
-                load_chunk(4)
-            else:
-                if k + 3 < NPART:
-                    hdn_t(k + 3, 0)
-                if k + 2 < NPART:
-                    t_out(k + 2, 1)
-            sq(k, 0)
-            sq(k, 1)
-            if k == 0:
-                t_out(2, 0)
-                t_out(2, 1)
-                cq(2)
-                cq(3)
-            else:
-                clamp_v(k - 1)
-            if k + 2 < NPART:
-                hq(k + 2)
-            if k >= 1 and 4 <= k + 2 <= 19:
-                cq(k + 2)
-            if chunk_work:
-                rg_v(k + 3)
-                rg_s(k + 3, 0)
-            mx(k, [2, 3])
-            if k >= 1:
-                sum_t(k - 1, [0, 1])
-            if k == 0:
-                hdn_t(3, 0)
-            elif k + 3 < NPART:
-                hdn_t(k + 3, 1)
-            if k + 3 < NPART:
-                t_out(k + 3, 0)
-            if k == 0:
-                hdn_t(3, 1)
-            sq(k, 2)
-            sq(k, 3)
-            if chunk_work:
-                rg_s(k + 3, 1)
-            for mm in range(4):
-                stt(k, mm)
-                if mm < 2:
-                    clamp_g(k, mm)
-            if k % 2 == 0:
-                if k // 2 + 4 <= 8:
-                    load_h(k // 2 + 4)
-                if k >= 2 and k // 2 + 4 <= 9:
-                    load_chunk(k // 2 + 4)
-            if k == 12:
-                nc.sync.dma_start(out=hb[:], in_=head_b.partition_broadcast(P))
-
         def ln_half(h):
             nc.scalar.activation(
                 out=lng[:, 512 * h : 512 * h + 512].rearrange("b (t p) -> b t p", t=4),
@@ -316,16 +230,126 @@ def tile_tokenmudule_pb_kernel(tc, hdn, fc2_w, fc2_b, head_w, head_b, out):
                 scale=1.0 / NT,
             )
 
-        clamp_v(NSTEP - 1)
-        sum_t(NSTEP - 2, [2, 3])
-        ln_half(0)
-        sum_t(NSTEP - 1, [0, 1])
-        sum_t(NSTEP - 1, [2, 3])
+        lts = {}
+
+        def ln_t(g):
+            lts[g] = bank(4 + g)
+            for j in range(4):
+                a = 4 * g + j
+                nc.tensor.transpose(
+                    out=lts[g][:, P * j : P * j + P], in_=lng[:, P * a : P * a + P], identity=ident_f[:]
+                )
+
+        nc.vector.memset(brow[:], 0.0)
+        nc.vector.memset(one[:], 1.0)
+        make_identity(nc, ident_f[:])
+        make_identity(nc, ident_b[:])
+        load_h(0, parts=2)
+        nc.scalar.dma_start(out=brow[0:8, :], in_=fc2_b.rearrange("(m p) -> m p", p=P))
+        load_chunk(0)
+        load_h(1)
+        load_chunk(1)
+        load_h(2)
+        load_chunk(2)
+
+        for i, (q, tp) in enumerate([(0, 0), (1, 0), (0, 1), (1, 1)]):
+            hdn_t(q, tp, [4, 5, 0, 1][i])
+            t_out(q, tp)
+        load_h(3)
+        load_chunk(3)
+        rg_v(0)
+        rg_s(0)
+        hq(0)
+        rg_v(1)
+        rg_s(1)
+        hq(1)
+        cq(0)
+        cq(1)
+
+        bt = psum.tile([P, P], BF16, name="bank3")
+        nc.tensor.transpose(out=bt[:], in_=brow[:], identity=ident_b[:])
+        nc.scalar.copy(out=bias[:], in_=bt[:, 0:8])
+
+        hdn_at = {0: [2, 3], 13: [16, 17]}
+        for k in range(1, 13):
+            hdn_at[k] = [k + 3]
+        rg_at = {0: [2], 1: [3], 15: [17, 18], 16: [19]}
+        for k in range(2, 15):
+            rg_at[k] = [k + 2]
+        cq_at = {1: [2], 2: []}
+        for k in range(3, 18):
+            cq_at[k] = rg_at[k - 1]
+        loads = {0: [("h", 4)], 1: [("c", 4)], 2: [("h", 5)], 3: [("c", 5)], 4: [("h", 6)], 5: [("c", 6)]}
+        loads.update({6: [("h", 7)], 7: [("c", 7)], 8: [("h", 8)], 9: [("c", 8)], 10: [("b", 0)], 11: [("c", 9)]})
+
+        for k in range(NSTEP):
+            hq_prev = hdn_at.get(k - 1, []) if k >= 2 else []
+            new_q = hdn_at.get(k, [])
+            mx(k)
+            if new_q:
+                hdn_t(new_q[0], 0, 4)
+                hdn_t(new_q[0], 1, 5)
+            if k == 0:
+                hdn_t(3, 0, 6)
+                hdn_t(3, 1, 7)
+            for mm in range(4):
+                sq(k, mm)
+            if new_q:
+                t_out(new_q[0], 0)
+                t_out(new_q[0], 1)
+            if k >= 1:
+                sum_t(k - 1)
+            if len(new_q) > 1:
+                if k > 0:
+                    hdn_t(new_q[1], 0, 4)
+                    hdn_t(new_q[1], 1, 5)
+                t_out(new_q[1], 0)
+                t_out(new_q[1], 1)
+            if k == NSTEP - 1:
+                ln_t(0)
+            if k == NSTEP - 1:
+                for r in cq_at[k]:
+                    cq(r)
+            last_g = 2 if k == NSTEP - 1 else G_TILES
+            for mm in range(4):
+                stt(k, mm)
+                if mm < last_g:
+                    clamp_g(k, mm)
+            for q in hq_prev:
+                hq(q)
+            for mm in range(last_g, 4):
+                clamp_v(k, mm)
+            if k < NSTEP - 1:
+                for r in cq_at.get(k, []):
+                    cq(r)
+            for r in rg_at.get(k, []):
+                rg_v(r)
+                rg_s(r)
+            if k == 0:
+                hq(2)
+                hq(3)
+            if k == 1:
+                cq(3)
+            for kind, i in loads.get(k, []):
+                if kind == "h":
+                    load_h(i)
+                elif kind == "c":
+                    load_chunk(i)
+                else:
+                    nc.sync.dma_start(out=hb[:], in_=head_b.partition_broadcast(P))
+            if k == NSTEP - 2:
+                ln_half(0)
+
+        sum_t(NSTEP - 1)
         ln_half(1)
+        ln_t(1)
 
         ps2 = {}
+        head_bank = [0, 1, 2, 3, 6, 7, 4, 5]
 
         def head_pass(nt, g):
+            if g == 0:
+                ps2[nt] = bank(head_bank[nt])
             nc.tensor.matmul_mx(
                 out=ps2[nt][:],
                 lhsT=g_codes[:, g, :].bitcast(FP8X4),
@@ -336,35 +360,25 @@ def tile_tokenmudule_pb_kernel(tc, hdn, fc2_w, fc2_b, head_w, head_b, out):
                 stop=(g == 1),
             )
 
-        lts = []
-        for g in range(2):
-            lt = ps_xt.tile([P, 4, P], F32, name="xt")
-            for j in range(4):
-                a = 4 * g + j
-                nc.tensor.transpose(out=lt[:, j, :], in_=lng[:, P * a : P * a + P], identity=ident_f[:])
-            lts.append(lt)
         for g in range(2):
             nc.scalar.activation(
-                out=g_grp[:, g, :, :], in_=lts[g][:].rearrange("p j b -> p b j"), func=ACT.Exp, scale=1.0 / 3.0
+                out=g_grp[:, g, :, :],
+                in_=lts[g][:].rearrange("p (j b) -> p b j", j=4),
+                func=ACT.Exp,
+                scale=1.0 / 3.0,
             )
             nc.vector.quantize_mx(
                 out=g_codes[:, g, :].bitcast(FP8X4),
                 scales=g_scales[:, g, :],
                 in_=g_grp[:, g, :, :].rearrange("p b j -> p (b j)"),
             )
-            if g == 0:
-                for nt in range(6):
-                    if nt < 4:
-                        ps2[nt] = ps_mm.tile([P, 512], F32, name="mm")
-                    else:
-                        ps2[nt] = ps_sum.tile([P, 512], F32, name="sum%d" % (nt - 4))
-                    head_pass(nt, 0)
         nc.scalar.activation(out=dmy[:], in_=one[:], func=ACT.Abs_reciprocal_sqrt)
+        head_pass(0, 0)
+        head_pass(1, 0)
         for nt in range(8):
-            if nt >= 6:
-                ps2[nt] = ps_xt.tile([P, 512], F32, name="xt")
-                head_pass(nt, 0)
             head_pass(nt, 1)
+            if nt + 2 < 8:
+                head_pass(nt + 2, 0)
         for nt in range(8):
             cols = slice(512 * nt, 512 * nt + 512)
             nc.vector.tensor_tensor(out=d[:, cols], in0=ps2[nt][:], in1=hb[:, cols], op=ALU.add)

@@ -162,9 +162,9 @@ def tile_tokenmudule_pb_kernel(tc, hdn, fc2_w, fc2_b, head_w, head_b, out):
                 hs[n] = hc_pool.tile([P, 2, 512], U8, name="hs", align_bytes=64)
             nc.vector.quantize_mx(out=hc[n][:, g, :].bitcast(FP8X4), scales=hs[n][:, g, :], in_=hg[n][:, g, :])
 
-        def mx(k):
+        def mx(k, mms):
             n, h = ORDER[k]
-            for mm in range(4):
+            for mm in mms:
                 ps = bank(mm)
                 for g in range(2):
                     nc.tensor.matmul_mx(
@@ -207,11 +207,11 @@ def tile_tokenmudule_pb_kernel(tc, hdn, fc2_w, fc2_b, head_w, head_b, out):
         def clamp_v(k, mm):
             nc.vector.tensor_scalar_max(out=c4[k][:, mm, :], in0=c4[k][:, mm, :], scalar1=EPS3)
 
-        def sum_t(k):
+        def sum_t(k, mms):
             n, h = ORDER[k]
-            if n == 0:
+            if n == 0 and mms[0] == 0:
                 sums[h] = bank(6 + h)
-            for mm in range(4):
+            for mm in mms:
                 for ts in range(4):
                     nc.tensor.matmul(
                         out=sums[h][:, P * mm : P * mm + P],
@@ -285,26 +285,22 @@ def tile_tokenmudule_pb_kernel(tc, hdn, fc2_w, fc2_b, head_w, head_b, out):
         for k in range(NSTEP):
             hq_prev = hdn_at.get(k - 1, []) if k >= 2 else []
             new_q = hdn_at.get(k, [])
-            mx(k)
-            if new_q:
-                hdn_t(new_q[0], 0, 4)
-                hdn_t(new_q[0], 1, 5)
-            if k == 0:
-                hdn_t(3, 0, 6)
-                hdn_t(3, 1, 7)
-            for mm in range(4):
-                sq(k, mm)
-            if new_q:
-                t_out(new_q[0], 0)
-                t_out(new_q[0], 1)
-            if k >= 1:
-                sum_t(k - 1)
+            for half in range(2):
+                mms = [2 * half, 2 * half + 1]
+                mx(k, mms)
+                if new_q:
+                    hdn_t(new_q[0], half, 4 + half)
+                for mm in mms:
+                    sq(k, mm)
+                if new_q:
+                    t_out(new_q[0], half)
+                if k >= 1:
+                    sum_t(k - 1, mms)
             if len(new_q) > 1:
-                if k > 0:
-                    hdn_t(new_q[1], 0, 4)
-                    hdn_t(new_q[1], 1, 5)
-                t_out(new_q[1], 0)
-                t_out(new_q[1], 1)
+                for half in range(2):
+                    hdn_t(new_q[1], half, (6 if k == 0 else 4) + half)
+                for half in range(2):
+                    t_out(new_q[1], half)
             if k == NSTEP - 1:
                 ln_t(0)
             if k == NSTEP - 1:
@@ -340,7 +336,7 @@ def tile_tokenmudule_pb_kernel(tc, hdn, fc2_w, fc2_b, head_w, head_b, out):
             if k == NSTEP - 2:
                 ln_half(0)
 
-        sum_t(NSTEP - 1)
+        sum_t(NSTEP - 1, [0, 1, 2, 3])
         ln_half(1)
         ln_t(1)
 

@@ -19,7 +19,8 @@ NCH = 1024
 NOUT = 4096
 EPS3 = 1e-18
 BIG = 3.0e38
-V_COLS = 288
+V_COLS = 256
+W_V_COLS = (352, 352, 512, 352)
 G_TILES = 3
 
 ORDER = (
@@ -58,6 +59,7 @@ def tile_tokenmudule_pb_kernel(tc, hdn, fc2_w, fc2_b, head_w, head_b, out):
         hw_scales = const.tile([P, 8, 2, 512], U8, align_bytes=64)
         hb = const.tile([P, NOUT], BF16)
         d = const.tile([P, NOUT], F32)
+        acc = const.tile([P, 2, 512], F32)
         junk = const.tile([P, 512], F32)
         lng = const.tile([P, NCH], F32)
         g_grp = const.tile([P, 2, P, 4], BF16, align_bytes=64)
@@ -112,14 +114,18 @@ def tile_tokenmudule_pb_kernel(tc, hdn, fc2_w, fc2_b, head_w, head_b, out):
                 in_=src.rearrange("p t (c i) -> p c t i", i=4),
             )
 
+        def v_cols(r):
+            return W_V_COLS[r] if r < 4 else V_COLS
+
         def rg_v(r):
             ci, g = divmod(r, 2)
             if g == 0:
                 grp[ci] = grp_pool.tile([P, 2, 512, 4], BF16, name="grp", align_bytes=64)
-            regroup(nc.vector.tensor_copy, r, 0, V_COLS)
+            regroup(nc.vector.tensor_copy, r, 0, v_cols(r))
 
         def rg_s(r):
-            regroup(nc.scalar.copy, r, V_COLS, 512)
+            if v_cols(r) < 512:
+                regroup(nc.scalar.copy, r, v_cols(r), 512)
 
         def cq(r):
             ci, g = divmod(r, 2)
@@ -162,13 +168,14 @@ def tile_tokenmudule_pb_kernel(tc, hdn, fc2_w, fc2_b, head_w, head_b, out):
                 hs[n] = hc_pool.tile([P, 2, 512], U8, name="hs", align_bytes=64)
             nc.vector.quantize_mx(out=hc[n][:, g, :].bitcast(FP8X4), scales=hs[n][:, g, :], in_=hg[n][:, g, :])
 
-        def mx(k, mms):
+        def mx(k, mms, gs=(0, 1)):
             n, h = ORDER[k]
             for mm in mms:
-                ps = bank(mm)
-                for g in range(2):
+                if gs[0] == 0:
+                    mm_ps[(k, mm)] = bank(mm)
+                for g in gs:
                     nc.tensor.matmul_mx(
-                        out=ps[:],
+                        out=mm_ps[(k, mm)][:],
                         lhsT=w_codes[:, h, g, P * mm : P * mm + P].bitcast(FP8X4),
                         lhsT_scale=w_scales[:, h, g, P * mm : P * mm + P],
                         rhs=hc[n][:, g, :].bitcast(FP8X4),
@@ -176,7 +183,6 @@ def tile_tokenmudule_pb_kernel(tc, hdn, fc2_w, fc2_b, head_w, head_b, out):
                         start=(g == 0),
                         stop=(g == 1),
                     )
-                mm_ps[(k, mm)] = ps
 
         def sq(k, mm):
             m = 4 * ORDER[k][1] + mm
@@ -204,18 +210,31 @@ def tile_tokenmudule_pb_kernel(tc, hdn, fc2_w, fc2_b, head_w, head_b, out):
                 out=c4[k][:, mm, :], in0=c4[k][:, mm, :], scalar1=BIG, scalar2=EPS3, op0=ALU.min, op1=ALU.max
             )
 
-        def clamp_v(k, mm):
-            nc.vector.tensor_scalar_max(out=c4[k][:, mm, :], in0=c4[k][:, mm, :], scalar1=EPS3)
+        def add_v(k):
+            n, h = ORDER[k]
+            if n == 0:
+                nc.vector.tensor_scalar_max(out=acc[:, h, :], in0=c4[k][:, 3, :], scalar1=EPS3)
+            else:
+                nc.vector.scalar_tensor_tensor(
+                    out=acc[:, h, :],
+                    in0=c4[k][:, 3, :],
+                    scalar=EPS3,
+                    in1=acc[:, h, :],
+                    op0=ALU.max,
+                    op1=ALU.add,
+                )
 
         def sum_t(k, mms):
             n, h = ORDER[k]
             if n == 0 and mms[0] == 0:
                 sums[h] = bank(6 + h)
             for mm in mms:
+                if mm == 3 and n < 8:
+                    continue
                 for ts in range(4):
                     nc.tensor.matmul(
                         out=sums[h][:, P * mm : P * mm + P],
-                        lhsT=c4[k][:, mm, P * ts : P * ts + P],
+                        lhsT=acc[:, h, P * ts : P * ts + P] if mm == 3 else c4[k][:, mm, P * ts : P * ts + P],
                         rhs=ident_f[:],
                         is_transpose=True,
                         start=(n == 0 and mm == 0 and ts == 0),
@@ -244,39 +263,39 @@ def tile_tokenmudule_pb_kernel(tc, hdn, fc2_w, fc2_b, head_w, head_b, out):
         nc.vector.memset(one[:], 1.0)
         make_identity(nc, ident_f[:])
         make_identity(nc, ident_b[:])
+        nc.sync.dma_start(out=brow[0:8, :], in_=fc2_b.rearrange("(m p) -> m p", p=P))
         load_h(0, parts=2)
-        nc.scalar.dma_start(out=brow[0:8, :], in_=fc2_b.rearrange("(m p) -> m p", p=P))
         load_chunk(0)
         load_h(1)
         load_chunk(1)
         load_h(2)
         load_chunk(2)
 
+        bt = psum.tile([P, P], BF16, name="bank3")
+        nc.tensor.transpose(out=bt[:], in_=brow[:], identity=ident_b[:])
+        nc.scalar.copy(out=bias[:], in_=bt[:, 0:8])
         for i, (q, tp) in enumerate([(0, 0), (1, 0), (0, 1), (1, 1)]):
             hdn_t(q, tp, [4, 5, 0, 1][i])
             t_out(q, tp)
         load_h(3)
-        load_chunk(3)
         rg_v(0)
         rg_s(0)
         hq(0)
+        cq(0)
         rg_v(1)
         rg_s(1)
         hq(1)
-        cq(0)
         cq(1)
+        load_chunk(3)
 
-        bt = psum.tile([P, P], BF16, name="bank3")
-        nc.tensor.transpose(out=bt[:], in_=brow[:], identity=ident_b[:])
-        nc.scalar.copy(out=bias[:], in_=bt[:, 0:8])
 
         hdn_at = {0: [2, 3], 13: [16, 17]}
         for k in range(1, 13):
             hdn_at[k] = [k + 3]
-        rg_at = {0: [2], 1: [3], 15: [17, 18], 16: [19]}
+        rg_at = {15: [17, 18], 16: [19]}
         for k in range(2, 15):
             rg_at[k] = [k + 2]
-        cq_at = {1: [2], 2: []}
+        cq_at = {1: [], 2: []}
         for k in range(3, 18):
             cq_at[k] = rg_at[k - 1]
         loads = {0: [("h", 4)], 1: [("c", 4)], 2: [("h", 5)], 3: [("c", 5)], 4: [("h", 6)], 5: [("c", 6)]}
@@ -285,47 +304,69 @@ def tile_tokenmudule_pb_kernel(tc, hdn, fc2_w, fc2_b, head_w, head_b, out):
         for k in range(NSTEP):
             hq_prev = hdn_at.get(k - 1, []) if k >= 2 else []
             new_q = hdn_at.get(k, [])
-            for half in range(2):
-                mms = [2 * half, 2 * half + 1]
-                mx(k, mms)
-                if new_q:
-                    hdn_t(new_q[0], half, 4 + half)
-                for mm in mms:
-                    sq(k, mm)
-                if new_q:
-                    t_out(new_q[0], half)
-                if k >= 1:
-                    sum_t(k - 1, mms)
-            if len(new_q) > 1:
-                for half in range(2):
-                    hdn_t(new_q[1], half, (6 if k == 0 else 4) + half)
-                for half in range(2):
-                    t_out(new_q[1], half)
-            if k == NSTEP - 1:
-                ln_t(0)
-            if k == NSTEP - 1:
-                for r in cq_at[k]:
-                    cq(r)
-            last_g = 2 if k == NSTEP - 1 else G_TILES
-            for mm in range(4):
-                stt(k, mm)
-                if mm < last_g:
-                    clamp_g(k, mm)
+            last = k == NSTEP - 1
             for q in hq_prev:
                 hq(q)
-            for mm in range(last_g, 4):
-                clamp_v(k, mm)
-            if k < NSTEP - 1:
-                for r in cq_at.get(k, []):
-                    cq(r)
-            for r in rg_at.get(k, []):
-                rg_v(r)
-                rg_s(r)
             if k == 0:
+                mx(0, [0, 1, 2, 3], [0])
+                for tp in range(2):
+                    hdn_t(2, tp, 4 + tp)
+                    t_out(2, tp)
+                mx(0, [0, 1, 2, 3], [1])
+                for tp in range(2):
+                    hdn_t(3, tp, 6 + tp)
+                rg_v(2)
                 hq(2)
-                hq(3)
-            if k == 1:
+                for mm in range(4):
+                    sq(0, mm)
+                    if mm == 1:
+                        t_out(3, 0)
+                        t_out(3, 1)
+                for mm in range(4):
+                    stt(0, mm)
+                    if mm < G_TILES:
+                        clamp_g(0, mm)
+                    if mm == 1:
+                        hq(3)
+                rg_s(2)
+                rg_v(3)
+                rg_s(3)
+                add_v(0)
+                cq(2)
                 cq(3)
+            else:
+                for half in range(2):
+                    mms = [2 * half, 2 * half + 1]
+                    mx(k, mms)
+                    if new_q:
+                        hdn_t(new_q[0], half, 4 + half)
+                    sum_t(k - 1, mms)
+                for mm in range(4):
+                    sq(k, mm)
+                if new_q:
+                    t_out(new_q[0], 0)
+                    t_out(new_q[0], 1)
+                if len(new_q) > 1:
+                    for half in range(2):
+                        hdn_t(new_q[1], half, 4 + half)
+                        t_out(new_q[1], half)
+                if last:
+                    ln_t(0)
+                    for r in cq_at[k]:
+                        cq(r)
+                for mm in range(4):
+                    stt(k, mm)
+                    if mm < (2 if last else G_TILES):
+                        clamp_g(k, mm)
+                if last:
+                    nc.vector.tensor_scalar_max(out=c4[k][:, 2, :], in0=c4[k][:, 2, :], scalar1=EPS3)
+                else:
+                    for r in cq_at.get(k, []):
+                        cq(r)
+                    for r in rg_at.get(k, []):
+                        rg_v(r)
+                        rg_s(r)
+                add_v(k)
             for kind, i in loads.get(k, []):
                 if kind == "h":
                     load_h(i)

@@ -115,7 +115,7 @@ def tile_tokenmudule_pb_kernel(tc, hdn, fc2_w, fc2_b, head_w, head_b, out):
             )
 
         def v_cols(r):
-            return W_V_COLS[r] if r < 4 else V_COLS
+            return W_V_COLS[r] if r < 4 else 512 if r == 19 else V_COLS
 
         def rg_v(r):
             ci, g = divmod(r, 2)
@@ -292,12 +292,8 @@ def tile_tokenmudule_pb_kernel(tc, hdn, fc2_w, fc2_b, head_w, head_b, out):
         hdn_at = {0: [2, 3], 13: [16, 17]}
         for k in range(1, 13):
             hdn_at[k] = [k + 3]
-        rg_at = {15: [17, 18], 16: [19]}
-        for k in range(2, 15):
-            rg_at[k] = [k + 2]
-        cq_at = {1: [], 2: []}
-        for k in range(3, 18):
-            cq_at[k] = rg_at[k - 1]
+        rg_at = {k: [k + 2] for k in range(2, 17)}
+        cq_at = {k: [k + 1] for k in range(3, 17)}
         loads = {0: [("h", 4)], 1: [("c", 4)], 2: [("h", 5)], 3: [("c", 5)], 4: [("h", 6)], 5: [("c", 6)]}
         loads.update({6: [("h", 7)], 7: [("c", 7)], 8: [("h", 8)], 9: [("c", 8)], 10: [("b", 0)], 11: [("c", 9)]})
 
@@ -351,9 +347,7 @@ def tile_tokenmudule_pb_kernel(tc, hdn, fc2_w, fc2_b, head_w, head_b, out):
                         hdn_t(new_q[1], half, 4 + half)
                         t_out(new_q[1], half)
                 if last:
-                    ln_t(0)
-                    for r in cq_at[k]:
-                        cq(r)
+                    ln_half(0)
                 for mm in range(4):
                     stt(k, mm)
                     if mm < (2 if last else G_TILES):
@@ -374,10 +368,12 @@ def tile_tokenmudule_pb_kernel(tc, hdn, fc2_w, fc2_b, head_w, head_b, out):
                     load_chunk(i)
                 else:
                     nc.sync.dma_start(out=hb[:], in_=head_b.partition_broadcast(P))
-            if k == NSTEP - 2:
-                ln_half(0)
 
+        cq(18)
+        rg_v(19)
+        cq(19)
         sum_t(NSTEP - 1, [0, 1, 2, 3])
+        ln_t(0)
         ln_half(1)
         ln_t(1)
 

@@ -19,14 +19,13 @@ NCH = 1024
 NOUT = 4096
 EPS3 = 1e-18
 BIG = 3.0e38
-V_COLS = 256
+V_COLS = 224
 W_V_COLS = (352, 352, 512, 352)
 G_TILES = 3
 
 ORDER = (
     [(0, 0), (1, 0), (0, 1), (1, 1)]
-    + [(n, h) for n in range(2, 7) for h in range(2)]
-    + [(7, 0), (8, 0), (7, 1), (8, 1)]
+    + [(n, h) for n in range(2, 9) for h in range(2)]
 )
 NSTEP = len(ORDER)
 
@@ -49,6 +48,7 @@ def tile_tokenmudule_pb_kernel(tc, hdn, fc2_w, fc2_b, head_w, head_b, out):
 
         ident_f = const.tile([P, P], F32)
         ident_b = const.tile([P, P], BF16)
+        zeros = const.tile([P, 512], BF16)
         brow = const.tile([P, P], BF16)
         bias = const.tile([P, 8], F32)
         one = const.tile([P, 1], F32)
@@ -65,7 +65,7 @@ def tile_tokenmudule_pb_kernel(tc, hdn, fc2_w, fc2_b, head_w, head_b, out):
         g_grp = const.tile([P, 2, P, 4], BF16, align_bytes=64)
         g_codes = const.tile([P, 2, P], U32, align_bytes=64)
         g_scales = const.tile([P, 2, P], U8, align_bytes=64)
-        ss = const.tile([P, 8], F32)
+        ss = const.tile([P, 9], F32)
         tot = const.tile([P, 1], F32)
         nrm = const.tile([P, 1], F32)
         rinv = const.tile([P, 1], F32)
@@ -84,6 +84,11 @@ def tile_tokenmudule_pb_kernel(tc, hdn, fc2_w, fc2_b, head_w, head_b, out):
         sums = {}
         s4 = {}
         c4 = {}
+
+        def keep_warm(b, count):
+            ps = bank(b)
+            for i in range(count):
+                nc.tensor.matmul(out=ps[:], lhsT=zeros[:, 0:P], rhs=zeros[:], start=True, stop=True)
 
         def load_h(n, parts=1):
             hr[n] = hr_pool.tile([P, 4, NF], BF16, name="hr")
@@ -186,7 +191,7 @@ def tile_tokenmudule_pb_kernel(tc, hdn, fc2_w, fc2_b, head_w, head_b, out):
 
         def sq(k, mm):
             m = 4 * ORDER[k][1] + mm
-            if mm == 0:
+            if k not in s4:
                 s4[k] = s_pool.tile([P, 4, 512], F32, name="s4")
             nc.scalar.activation(
                 out=s4[k][:, mm, :], in_=mm_ps[(k, mm)][:], func=ACT.Square, bias=bias[:, m : m + 1], scale=1.0
@@ -194,7 +199,7 @@ def tile_tokenmudule_pb_kernel(tc, hdn, fc2_w, fc2_b, head_w, head_b, out):
 
         def stt(k, mm):
             m = 4 * ORDER[k][1] + mm
-            if mm == 0:
+            if k not in c4:
                 c4[k] = c_pool.tile([P, 4, 512], F32, name="c4")
             nc.vector.scalar_tensor_tensor(
                 out=c4[k][:, mm, :],
@@ -224,27 +229,31 @@ def tile_tokenmudule_pb_kernel(tc, hdn, fc2_w, fc2_b, head_w, head_b, out):
                     op1=ALU.add,
                 )
 
+        def sum_blocks(h, mm, tile, start=False, stop=False):
+            for ts in range(4):
+                nc.tensor.matmul(
+                    out=sums[h][:, P * mm : P * mm + P],
+                    lhsT=tile[:, P * ts : P * ts + P],
+                    rhs=ident_f[:],
+                    is_transpose=True,
+                    start=(start and ts == 0),
+                    stop=(stop and ts == 3),
+                )
+
         def sum_t(k, mms):
             n, h = ORDER[k]
             if n == 0 and mms[0] == 0:
                 sums[h] = bank(6 + h)
             for mm in mms:
-                if mm == 3 and n < 8:
-                    continue
-                for ts in range(4):
-                    nc.tensor.matmul(
-                        out=sums[h][:, P * mm : P * mm + P],
-                        lhsT=acc[:, h, P * ts : P * ts + P] if mm == 3 else c4[k][:, mm, P * ts : P * ts + P],
-                        rhs=ident_f[:],
-                        is_transpose=True,
-                        start=(n == 0 and mm == 0 and ts == 0),
-                        stop=(n == 8 and mm == 3 and ts == 3),
-                    )
+                if mm < 3:
+                    sum_blocks(h, mm, c4[k][:, mm, :], start=(n == 0 and mm == 0))
+                elif n == 8 and h == 0:
+                    sum_blocks(h, 3, acc[:, h, :], stop=True)
 
-        def ln_half(h):
+        def ln_part(h, m0, m1):
             nc.scalar.activation(
-                out=lng[:, 512 * h : 512 * h + 512].rearrange("b (t p) -> b t p", t=4),
-                in_=sums[h][:].rearrange("b (p t) -> b t p", t=4),
+                out=lng[:, 512 * h : 512 * h + 512].rearrange("b (t p) -> b t p", t=4)[:, :, 32 * m0 : 32 * m1],
+                in_=sums[h][:, P * m0 : P * m1].rearrange("b (p t) -> b t p", t=4),
                 func=ACT.Ln,
                 scale=1.0 / NT,
             )
@@ -260,7 +269,9 @@ def tile_tokenmudule_pb_kernel(tc, hdn, fc2_w, fc2_b, head_w, head_b, out):
                 )
 
         nc.vector.memset(brow[:], 0.0)
+        nc.vector.memset(zeros[:], 0.0)
         nc.vector.memset(one[:], 1.0)
+        nc.scalar.activation(out=dmy[:], in_=one[:], func=ACT.Ln)
         make_identity(nc, ident_f[:])
         make_identity(nc, ident_b[:])
         nc.sync.dma_start(out=brow[0:8, :], in_=fc2_b.rearrange("(m p) -> m p", p=P))
@@ -271,12 +282,14 @@ def tile_tokenmudule_pb_kernel(tc, hdn, fc2_w, fc2_b, head_w, head_b, out):
         load_h(2)
         load_chunk(2)
 
+        keep_warm(2, 6)
         bt = psum.tile([P, P], BF16, name="bank3")
         nc.tensor.transpose(out=bt[:], in_=brow[:], identity=ident_b[:])
         nc.scalar.copy(out=bias[:], in_=bt[:, 0:8])
         for i, (q, tp) in enumerate([(0, 0), (1, 0), (0, 1), (1, 1)]):
             hdn_t(q, tp, [4, 5, 0, 1][i])
             t_out(q, tp)
+        keep_warm(2, 6)
         load_h(3)
         rg_v(0)
         rg_s(0)
@@ -289,11 +302,11 @@ def tile_tokenmudule_pb_kernel(tc, hdn, fc2_w, fc2_b, head_w, head_b, out):
         load_chunk(3)
 
 
-        hdn_at = {0: [2, 3], 13: [16, 17]}
-        for k in range(1, 13):
+        hdn_at = {0: [2, 3]}
+        for k in range(1, 15):
             hdn_at[k] = [k + 3]
         rg_at = {k: [k + 2] for k in range(2, 17)}
-        cq_at = {k: [k + 1] for k in range(3, 17)}
+        cq_at = {k: [k + 1] for k in range(3, 16)}
         loads = {0: [("h", 4)], 1: [("c", 4)], 2: [("h", 5)], 3: [("c", 5)], 4: [("h", 6)], 5: [("c", 6)]}
         loads.update({6: [("h", 7)], 7: [("c", 7)], 8: [("h", 8)], 9: [("c", 8)], 10: [("b", 0)], 11: [("c", 9)]})
 
@@ -331,36 +344,32 @@ def tile_tokenmudule_pb_kernel(tc, hdn, fc2_w, fc2_b, head_w, head_b, out):
                 cq(2)
                 cq(3)
             else:
+                tiles = [0, 1, 2, 3]
                 for half in range(2):
-                    mms = [2 * half, 2 * half + 1]
-                    mx(k, mms)
+                    mx(k, tiles[2 * half : 2 * half + 2])
                     if new_q:
                         hdn_t(new_q[0], half, 4 + half)
-                    sum_t(k - 1, mms)
-                for mm in range(4):
+                    sum_t(k - 1, [2 * half, 2 * half + 1])
+                for mm in tiles:
                     sq(k, mm)
                 if new_q:
                     t_out(new_q[0], 0)
                     t_out(new_q[0], 1)
-                if len(new_q) > 1:
-                    for half in range(2):
-                        hdn_t(new_q[1], half, 4 + half)
-                        t_out(new_q[1], half)
                 if last:
-                    ln_half(0)
-                for mm in range(4):
+                    ln_part(0, 0, 4)
+                for mm in tiles:
                     stt(k, mm)
-                    if mm < (2 if last else G_TILES):
+                    if mm < G_TILES:
                         clamp_g(k, mm)
                 if last:
-                    nc.vector.tensor_scalar_max(out=c4[k][:, 2, :], in0=c4[k][:, 2, :], scalar1=EPS3)
+                    nc.vector.tensor_scalar_max(out=c4[k][:, 3, :], in0=c4[k][:, 3, :], scalar1=EPS3)
                 else:
                     for r in cq_at.get(k, []):
                         cq(r)
                     for r in rg_at.get(k, []):
                         rg_v(r)
                         rg_s(r)
-                add_v(k)
+                    add_v(k)
             for kind, i in loads.get(k, []):
                 if kind == "h":
                     load_h(i)
@@ -369,13 +378,18 @@ def tile_tokenmudule_pb_kernel(tc, hdn, fc2_w, fc2_b, head_w, head_b, out):
                 else:
                     nc.sync.dma_start(out=hb[:], in_=head_b.partition_broadcast(P))
 
+        cq(17)
         cq(18)
         rg_v(19)
         cq(19)
-        sum_t(NSTEP - 1, [0, 1, 2, 3])
+        sum_blocks(1, 3, acc[:, 1, :])
+        sum_t(NSTEP - 1, [0, 1, 2])
+        sum_blocks(1, 3, c4[NSTEP - 1][:, 3, :], stop=True)
         ln_t(0)
-        ln_half(1)
+        ln_part(1, 0, 2)
+        ln_part(1, 2, 4)
         ln_t(1)
+        keep_warm(0, 4)
 
         ps2 = {}
         head_bank = [0, 1, 2, 3, 6, 7, 4, 5]
@@ -412,11 +426,14 @@ def tile_tokenmudule_pb_kernel(tc, hdn, fc2_w, fc2_b, head_w, head_b, out):
             head_pass(nt, 1)
             if nt + 2 < 8:
                 head_pass(nt + 2, 0)
-        for nt in range(8):
-            cols = slice(512 * nt, 512 * nt + 512)
-            nc.vector.tensor_tensor(out=d[:, cols], in0=ps2[nt][:], in1=hb[:, cols], op=ALU.add)
-            nc.scalar.activation(out=junk[:], in_=d[:, cols], func=ACT.Square, accum_out=ss[:, nt : nt + 1])
-        nc.scalar.activation(out=junk[:, 0:8], in_=ss[:], func=ACT.Identity, accum_out=tot[:])
+        parts = [(nt, 0, 512) for nt in range(7)] + [(7, 0, 256), (7, 256, 512)]
+        for i, (nt, n0, n1) in enumerate(parts):
+            cols = slice(512 * nt + n0, 512 * nt + n1)
+            nc.vector.tensor_tensor(out=d[:, cols], in0=ps2[nt][:, n0:n1], in1=hb[:, cols], op=ALU.add)
+            nc.scalar.activation(
+                out=junk[:, 0 : n1 - n0], in_=d[:, cols], func=ACT.Square, accum_out=ss[:, i : i + 1]
+            )
+        nc.scalar.activation(out=junk[:, 0:9], in_=ss[:], func=ACT.Identity, accum_out=tot[:])
         nc.scalar.activation(out=nrm[:], in_=tot[:], func=ACT.Abs_reciprocal_sqrt)
         nc.vector.tensor_scalar_min(out=rinv[:], in0=nrm[:], scalar1=1e12)
         for nt in range(8):

@@ -10,6 +10,7 @@ U8 = mybir.dt.uint8
 FP8X4 = mybir.dt.float8_e4m3fn_x4
 ALU = mybir.AluOpType
 ACT = mybir.ActivationFunctionType
+AX = mybir.AxisListType
 
 P = 128
 NB = 128
@@ -21,6 +22,7 @@ EPS3 = 1e-18
 BIG = 3.0e38
 V_COLS = 224
 W_V_COLS = (352, 352, 512, 352)
+LATE_V_COLS = {17: 128, 18: 288, 19: 512}
 G_TILES = 3
 
 ORDER = (
@@ -66,7 +68,7 @@ def tile_tokenmudule_pb_kernel(tc, hdn, fc2_w, fc2_b, head_w, head_b, out):
         g_codes = const.tile([P, 2, P], U32, align_bytes=64)
         g_scales = const.tile([P, 2, P], U8, align_bytes=64)
         ss = const.tile([P, 9], F32)
-        tot = const.tile([P, 1], F32)
+        part = const.tile([P, 1], F32)
         nrm = const.tile([P, 1], F32)
         rinv = const.tile([P, 1], F32)
 
@@ -120,7 +122,7 @@ def tile_tokenmudule_pb_kernel(tc, hdn, fc2_w, fc2_b, head_w, head_b, out):
             )
 
         def v_cols(r):
-            return W_V_COLS[r] if r < 4 else 512 if r == 19 else V_COLS
+            return W_V_COLS[r] if r < 4 else LATE_V_COLS.get(r, V_COLS)
 
         def rg_v(r):
             ci, g = divmod(r, 2)
@@ -305,7 +307,7 @@ def tile_tokenmudule_pb_kernel(tc, hdn, fc2_w, fc2_b, head_w, head_b, out):
         hdn_at = {0: [2, 3]}
         for k in range(1, 15):
             hdn_at[k] = [k + 3]
-        rg_at = {k: [k + 2] for k in range(2, 17)}
+        rg_at = {k: [k + 2] for k in range(2, 16)}
         cq_at = {k: [k + 1] for k in range(3, 16)}
         loads = {0: [("h", 4)], 1: [("c", 4)], 2: [("h", 5)], 3: [("c", 5)], 4: [("h", 6)], 5: [("c", 6)]}
         loads.update({6: [("h", 7)], 7: [("c", 7)], 8: [("h", 8)], 9: [("c", 8)], 10: [("b", 0)], 11: [("c", 9)]})
@@ -379,9 +381,10 @@ def tile_tokenmudule_pb_kernel(tc, hdn, fc2_w, fc2_b, head_w, head_b, out):
                     nc.sync.dma_start(out=hb[:], in_=head_b.partition_broadcast(P))
 
         cq(17)
-        cq(18)
+        rg_v(18)
+        rg_s(18)
         rg_v(19)
-        cq(19)
+        cq(18)
         sum_blocks(1, 3, acc[:, 1, :])
         sum_t(NSTEP - 1, [0, 1, 2])
         sum_blocks(1, 3, c4[NSTEP - 1][:, 3, :], stop=True)
@@ -419,6 +422,7 @@ def tile_tokenmudule_pb_kernel(tc, hdn, fc2_w, fc2_b, head_w, head_b, out):
                 scales=g_scales[:, g, :],
                 in_=g_grp[:, g, :, :].rearrange("p b j -> p (b j)"),
             )
+        cq(19)
         nc.scalar.activation(out=dmy[:], in_=one[:], func=ACT.Abs_reciprocal_sqrt)
         head_pass(0, 0)
         head_pass(1, 0)
@@ -433,12 +437,14 @@ def tile_tokenmudule_pb_kernel(tc, hdn, fc2_w, fc2_b, head_w, head_b, out):
             nc.scalar.activation(
                 out=junk[:, 0 : n1 - n0], in_=d[:, cols], func=ACT.Square, accum_out=ss[:, i : i + 1]
             )
-        nc.scalar.activation(out=junk[:, 0:9], in_=ss[:], func=ACT.Identity, accum_out=tot[:])
-        nc.scalar.activation(out=nrm[:], in_=tot[:], func=ACT.Abs_reciprocal_sqrt)
+            if i == 8:
+                nc.vector.reduce_sum(out=part[:], in_=ss[:, 0:8], axis=AX.X)
+        nc.scalar.activation(out=nrm[:], in_=ss[:, 8:9], func=ACT.Abs_reciprocal_sqrt, bias=part[:, 0:1])
         nc.vector.tensor_scalar_min(out=rinv[:], in0=nrm[:], scalar1=1e12)
-        for nt in range(8):
-            cols = slice(512 * nt, 512 * nt + 512)
-            if nt % 3 == 1:
+        edges = [0, 256] + [512 * i for i in range(1, 9)]
+        for i in range(len(edges) - 1):
+            cols = slice(edges[i], edges[i + 1])
+            if i % 3 == 2:
                 nc.scalar.activation(out=d[:, cols], in_=d[:, cols], func=ACT.Copy, scale=rinv[:, 0:1])
             else:
                 nc.vector.tensor_scalar_mul(out=d[:, cols], in0=d[:, cols], scalar1=rinv[:, 0:1])

from contextlib import ExitStack

import concourse.mybir as mybir
from concourse.masks import make_identity

F32 = mybir.dt.float32
BF16 = mybir.dt.bfloat16
U32 = mybir.dt.uint32
U8 = mybir.dt.uint8
FP8X4 = mybir.dt.float8_e4m3fn_x4
ALU = mybir.AluOpType
ACT = mybir.ActivationFunctionType
AX = mybir.AxisListType

P = 128
NB = 128
NT = 36
NF = 1024
NCH = 1024
NOUT = 4096
EPS3 = 1e-18
BIG = 3.0e38
V_COLS = 224
W_V_COLS = (352, 352, 512, 352)
LATE_V_COLS = {17: 128, 18: 288, 19: 512}
G_TILES = 3

ORDER = (
    [(0, 0), (1, 0), (0, 1), (1, 1)]
    + [(n, h) for n in range(2, 9) for h in range(2)]
)
NSTEP = len(ORDER)

FLOPS = 2 * NB * NT * NF * NCH + 2 * NB * NCH * NOUT


def tile_tokenmudule_pb_kernel(tc, hdn, fc2_w, fc2_b, head_w, head_b, out):
    nc = tc.nc
    with ExitStack() as ctx:
        const = ctx.enter_context(tc.tile_pool(name="const", bufs=1))
        hr_pool = ctx.enter_context(tc.tile_pool(name="hr", bufs=3))
        hg_pool = ctx.enter_context(tc.tile_pool(name="hg", bufs=2))
        hc_pool = ctx.enter_context(tc.tile_pool(name="hc", bufs=3))
        raw_pool = ctx.enter_context(tc.tile_pool(name="raw", bufs=3))
        grp_pool = ctx.enter_context(tc.tile_pool(name="grp", bufs=2))
        s_pool = ctx.enter_context(tc.tile_pool(name="sq", bufs=2))
        c_pool = ctx.enter_context(tc.tile_pool(name="cube", bufs=3))
        psum = ctx.enter_context(tc.psum_pool(name="psum", bufs=1))
        ctx.enter_context(tc.manual_schedule())

        ident_f = const.tile([P, P], F32)
        ident_b = const.tile([P, P], BF16)
        zeros = const.tile([P, 512], BF16)
        brow = const.tile([P, P], BF16)
        bias = const.tile([P, 8], F32)
        one = const.tile([P, 1], F32)
        dmy = const.tile([P, 1], F32)
        w_codes = const.tile([P, 2, 2, 512], U32, align_bytes=64)
        w_scales = const.tile([P, 2, 2, 512], U8, align_bytes=64)
        hw_codes = const.tile([P, 8, 2, 512], U32, align_bytes=64)
        hw_scales = const.tile([P, 8, 2, 512], U8, align_bytes=64)
        hb = const.tile([P, NOUT], BF16)
        d = const.tile([P, NOUT], F32)
        acc = const.tile([P, 2, 512], F32)
        junk = const.tile([P, 512], F32)
        lng = const.tile([P, NCH], F32)
        g_grp = const.tile([P, 2, P, 4], BF16, align_bytes=64)
        g_codes = const.tile([P, 2, P], U32, align_bytes=64)
        g_scales = const.tile([P, 2, P], U8, align_bytes=64)
        ss = const.tile([P, 9], F32)
        part = const.tile([P, 1], F32)
        nrm = const.tile([P, 1], F32)
        rinv = const.tile([P, 1], F32)

        def bank(i):
            return psum.tile([P, 512], F32, name="bank%d" % i)

        hr = {}
        hg = {}
        hc = {}
        hs = {}
        raw = {}
        grp = {}
        xts = {}
        mm_ps = {}
        sums = {}
        s4 = {}
        c4 = {}

        def keep_warm(b, count):
            ps = bank(b)
            for i in range(count):
                nc.tensor.matmul(out=ps[:], lhsT=zeros[:, 0:P], rhs=zeros[:], start=True, stop=True)

        def load_h(n, parts=1):
            hr[n] = hr_pool.tile([P, 4, NF], BF16, name="hr")
            w = 4 // parts
            for i in range(parts):
                nc.sync.dma_start(
                    out=hr[n][:, w * i : w * i + w, :], in_=hdn[:, 4 * n + w * i : 4 * n + w * i + w, :]
                )

        def load_chunk(ci):
            raw[ci] = raw_pool.tile([P, 8, 512], BF16, name="raw")
            if ci < 2:
                src = fc2_w[:, 512 * ci : 512 * ci + 512]
            else:
                src = head_w[:, 512 * (ci - 2) : 512 * (ci - 2) + 512]
            for g in range(2):
                nc.sync.dma_start(
                    out=raw[ci][:, 4 * g : 4 * g + 4, :],
                    in_=src[512 * g : 512 * g + 512, :].rearrange("(p t) c -> p t c", t=4),
                )

        def regroup(eng_copy, r, n0, n1):
            ci, g = divmod(r, 2)
            src = raw[ci][:, 4 * g : 4 * g + 4, n0:n1]
            dst = grp[ci][:, g, n0:n1, :]
            eng_copy(
                out=dst.rearrange("p (c i) t -> p c t i", i=4),
                in_=src.rearrange("p t (c i) -> p c t i", i=4),
            )

        def v_cols(r):
            return W_V_COLS[r] if r < 4 else LATE_V_COLS.get(r, V_COLS)

        def rg_v(r):
            ci, g = divmod(r, 2)
            if g == 0:
                grp[ci] = grp_pool.tile([P, 2, 512, 4], BF16, name="grp", align_bytes=64)
            regroup(nc.vector.tensor_copy, r, 0, v_cols(r))

        def rg_s(r):
            if v_cols(r) < 512:
                regroup(nc.scalar.copy, r, v_cols(r), 512)

        def cq(r):
            ci, g = divmod(r, 2)
            if ci < 2:
                codes, scales = w_codes[:, ci, g, :], w_scales[:, ci, g, :]
            else:
                codes, scales = hw_codes[:, ci - 2, g, :], hw_scales[:, ci - 2, g, :]
            nc.vector.quantize_mx(
                out=codes.bitcast(FP8X4),
                scales=scales,
                in_=grp[ci][:, g, :, :].rearrange("p n j -> p (n j)"),
            )

        def hdn_t(q, tp, b):
            n, g = divmod(q, 2)
            xt = bank(b)
            for u in range(2):
                for t2 in range(2):
                    nc.tensor.transpose(
                        out=xt[:, 256 * u + P * t2 : 256 * u + P * t2 + P],
                        in_=hr[n][:, 2 * tp + t2, :].bitcast(F32)[:, 256 * g + u : 256 * g + 256 : 2],
                        identity=ident_f[:],
                    )
            xts[(q, tp)] = xt

        def t_out(q, tp):
            n, g = divmod(q, 2)
            if n not in hg:
                hg[n] = hg_pool.tile([P, 2, 2048], BF16, name="hg", align_bytes=64)
            g32 = hg[n][:, g, :].bitcast(F32)
            nc.scalar.copy(
                out=g32[:, 512 * tp : 512 * tp + 512].rearrange("p (c u) -> p c u", u=2),
                in_=xts[(q, tp)][:].rearrange("p (u c) -> p c u", u=2),
            )

        def hq(q):
            n, g = divmod(q, 2)
            if g == 0:
                hc[n] = hc_pool.tile([P, 2, 512], U32, name="hc", align_bytes=64)
                hs[n] = hc_pool.tile([P, 2, 512], U8, name="hs", align_bytes=64)
            nc.vector.quantize_mx(out=hc[n][:, g, :].bitcast(FP8X4), scales=hs[n][:, g, :], in_=hg[n][:, g, :])

        def mx(k, mms, gs=(0, 1)):
            n, h = ORDER[k]
            for mm in mms:
                if gs[0] == 0:
                    mm_ps[(k, mm)] = bank(mm)
                for g in gs:
                    nc.tensor.matmul_mx(
                        out=mm_ps[(k, mm)][:],
                        lhsT=w_codes[:, h, g, P * mm : P * mm + P].bitcast(FP8X4),
                        lhsT_scale=w_scales[:, h, g, P * mm : P * mm + P],
                        rhs=hc[n][:, g, :].bitcast(FP8X4),
                        rhs_scale=hs[n][:, g, :],
                        start=(g == 0),
                        stop=(g == 1),
                    )

        def sq(k, mm):
            m = 4 * ORDER[k][1] + mm
            if k not in s4:
                s4[k] = s_pool.tile([P, 4, 512], F32, name="s4")
            nc.scalar.activation(
                out=s4[k][:, mm, :], in_=mm_ps[(k, mm)][:], func=ACT.Square, bias=bias[:, m : m + 1], scale=1.0
            )

        def stt(k, mm):
            m = 4 * ORDER[k][1] + mm
            if k not in c4:
                c4[k] = c_pool.tile([P, 4, 512], F32, name="c4")
            nc.vector.scalar_tensor_tensor(
                out=c4[k][:, mm, :],
                in0=mm_ps[(k, mm)][:],
                scalar=bias[:, m : m + 1],
                in1=s4[k][:, mm, :],
                op0=ALU.add,
                op1=ALU.mult,
            )

        def clamp_g(k, mm):
            nc.gpsimd.tensor_scalar(
                out=c4[k][:, mm, :], in0=c4[k][:, mm, :], scalar1=BIG, scalar2=EPS3, op0=ALU.min, op1=ALU.max
            )

        def add_v(k):
            n, h = ORDER[k]
            if n == 0:
                nc.vector.tensor_scalar_max(out=acc[:, h, :], in0=c4[k][:, 3, :], scalar1=EPS3)
            else:
                nc.vector.scalar_tensor_tensor(
                    out=acc[:, h, :],
                    in0=c4[k][:, 3, :],
                    scalar=EPS3,
                    in1=acc[:, h, :],
                    op0=ALU.max,
                    op1=ALU.add,
                )

        def sum_blocks(h, mm, tile, start=False, stop=False):
            for ts in range(4):
                nc.tensor.matmul(
                    out=sums[h][:, P * mm : P * mm + P],
                    lhsT=tile[:, P * ts : P * ts + P],
                    rhs=ident_f[:],
                    is_transpose=True,
                    start=(start and ts == 0),
                    stop=(stop and ts == 3),
                )

        def sum_t(k, mms):
            n, h = ORDER[k]
            if n == 0 and mms[0] == 0:
                sums[h] = bank(6 + h)
            for mm in mms:
                if mm < 3:
                    sum_blocks(h, mm, c4[k][:, mm, :], start=(n == 0 and mm == 0))
                elif n == 8 and h == 0:
                    sum_blocks(h, 3, acc[:, h, :], stop=True)

        def ln_part(h, m0, m1):
            nc.scalar.activation(
                out=lng[:, 512 * h : 512 * h + 512].rearrange("b (t p) -> b t p", t=4)[:, :, 32 * m0 : 32 * m1],
                in_=sums[h][:, P * m0 : P * m1].rearrange("b (p t) -> b t p", t=4),
                func=ACT.Ln,
                scale=1.0 / NT,
            )

        lts = {}

        def ln_t(g):
            lts[g] = bank(4 + g)
            for j in range(4):
                a = 4 * g + j
                nc.tensor.transpose(
                    out=lts[g][:, P * j : P * j + P], in_=lng[:, P * a : P * a + P], identity=ident_f[:]
                )

        nc.vector.memset(brow[:], 0.0)
        nc.vector.memset(zeros[:], 0.0)
        nc.vector.memset(one[:], 1.0)
        nc.scalar.activation(out=dmy[:], in_=one[:], func=ACT.Ln)
        make_identity(nc, ident_f[:])
        make_identity(nc, ident_b[:])
        nc.sync.dma_start(out=brow[0:8, :], in_=fc2_b.rearrange("(m p) -> m p", p=P))
        load_h(0, parts=2)
        load_chunk(0)
        load_h(1)
        load_chunk(1)
        load_h(2)
        load_chunk(2)

        keep_warm(2, 6)
        bt = psum.tile([P, P], BF16, name="bank3")
        nc.tensor.transpose(out=bt[:], in_=brow[:], identity=ident_b[:])
        nc.scalar.copy(out=bias[:], in_=bt[:, 0:8])
        for i, (q, tp) in enumerate([(0, 0), (1, 0), (0, 1), (1, 1)]):
            hdn_t(q, tp, [4, 5, 0, 1][i])
            t_out(q, tp)
        keep_warm(2, 6)
        load_h(3)
        rg_v(0)
        rg_s(0)
        hq(0)
        cq(0)
        rg_v(1)
        rg_s(1)
        hq(1)
        cq(1)
        load_chunk(3)


        hdn_at = {0: [2, 3]}
        for k in range(1, 15):
            hdn_at[k] = [k + 3]
        rg_at = {k: [k + 2] for k in range(2, 16)}
        cq_at = {k: [k + 1] for k in range(3, 16)}
        loads = {0: [("h", 4)], 1: [("c", 4)], 2: [("h", 5)], 3: [("c", 5)], 4: [("h", 6)], 5: [("c", 6)]}
        loads.update({6: [("h", 7)], 7: [("c", 7)], 8: [("h", 8)], 9: [("c", 8)], 10: [("b", 0)], 11: [("c", 9)]})

        for k in range(NSTEP):
            hq_prev = hdn_at.get(k - 1, []) if k >= 2 else []
            new_q = hdn_at.get(k, [])
            last = k == NSTEP - 1
            for q in hq_prev:
                hq(q)
            if k == 0:
                mx(0, [0, 1, 2, 3], [0])
                for tp in range(2):
                    hdn_t(2, tp, 4 + tp)
                    t_out(2, tp)
                mx(0, [0, 1, 2, 3], [1])
                for tp in range(2):
                    hdn_t(3, tp, 6 + tp)
                rg_v(2)
                hq(2)
                for mm in range(4):
                    sq(0, mm)
                    if mm == 1:
                        t_out(3, 0)
                        t_out(3, 1)
                for mm in range(4):
                    stt(0, mm)
                    if mm < G_TILES:
                        clamp_g(0, mm)
                    if mm == 1:
                        hq(3)
                rg_s(2)
                rg_v(3)
                rg_s(3)
                add_v(0)
                cq(2)
                cq(3)
            else:
                tiles = [0, 1, 2, 3]
                for half in range(2):
                    mx(k, tiles[2 * half : 2 * half + 2])
                    if new_q:
                        hdn_t(new_q[0], half, 4 + half)
                    sum_t(k - 1, [2 * half, 2 * half + 1])
                for mm in tiles:
                    sq(k, mm)
                if new_q:
                    t_out(new_q[0], 0)
                    t_out(new_q[0], 1)
                if last:
                    ln_part(0, 0, 4)
                for mm in tiles:
                    stt(k, mm)
                    if mm < G_TILES:
                        clamp_g(k, mm)
                if last:
                    nc.vector.tensor_scalar_max(out=c4[k][:, 3, :], in0=c4[k][:, 3, :], scalar1=EPS3)
                else:
                    for r in cq_at.get(k, []):
                        cq(r)
                    for r in rg_at.get(k, []):
                        rg_v(r)
                        rg_s(r)
                    add_v(k)
            for kind, i in loads.get(k, []):
                if kind == "h":
                    load_h(i)
                elif kind == "c":
                    load_chunk(i)
                else:
                    nc.sync.dma_start(out=hb[:], in_=head_b.partition_broadcast(P))

        cq(17)
        rg_v(18)
        rg_s(18)
        rg_v(19)
        cq(18)
        sum_blocks(1, 3, acc[:, 1, :])
        sum_t(NSTEP - 1, [0, 1, 2])
        sum_blocks(1, 3, c4[NSTEP - 1][:, 3, :], stop=True)
        ln_t(0)
        ln_part(1, 0, 2)
        ln_part(1, 2, 4)
        ln_t(1)
        keep_warm(0, 4)

        ps2 = {}
        head_bank = [0, 1, 2, 3, 6, 7, 4, 5]

        def head_pass(nt, g):
            if g == 0:
                ps2[nt] = bank(head_bank[nt])
            nc.tensor.matmul_mx(
                out=ps2[nt][:],
                lhsT=g_codes[:, g, :].bitcast(FP8X4),
                lhsT_scale=g_scales[:, g, :],
                rhs=hw_codes[:, nt, g, :].bitcast(FP8X4),
                rhs_scale=hw_scales[:, nt, g, :],
                start=(g == 0),
                stop=(g == 1),
            )

        for g in range(2):
            nc.scalar.activation(
                out=g_grp[:, g, :, :],
                in_=lts[g][:].rearrange("p (j b) -> p b j", j=4),
                func=ACT.Exp,
                scale=1.0 / 3.0,
            )
            nc.vector.quantize_mx(
                out=g_codes[:, g, :].bitcast(FP8X4),
                scales=g_scales[:, g, :],
                in_=g_grp[:, g, :, :].rearrange("p b j -> p (b j)"),
            )
        cq(19)
        nc.scalar.activation(out=dmy[:], in_=one[:], func=ACT.Abs_reciprocal_sqrt)
        head_pass(0, 0)
        head_pass(1, 0)
        for nt in range(8):
            head_pass(nt, 1)
            if nt + 2 < 8:
                head_pass(nt + 2, 0)
        parts = [(nt, 0, 512) for nt in range(7)] + [(7, 0, 256), (7, 256, 512)]
        for i, (nt, n0, n1) in enumerate(parts):
            cols = slice(512 * nt + n0, 512 * nt + n1)
            nc.vector.tensor_tensor(out=d[:, cols], in0=ps2[nt][:, n0:n1], in1=hb[:, cols], op=ALU.add)
            nc.scalar.activation(
                out=junk[:, 0 : n1 - n0], in_=d[:, cols], func=ACT.Square, accum_out=ss[:, i : i + 1]
            )
            if i == 8:
                nc.vector.reduce_sum(out=part[:], in_=ss[:, 0:8], axis=AX.X)
        nc.scalar.activation(out=nrm[:], in_=ss[:, 8:9], func=ACT.Abs_reciprocal_sqrt, bias=part[:, 0:1])
        nc.vector.tensor_scalar_min(out=rinv[:], in0=nrm[:], scalar1=1e12)
        edges = [0, 256] + [512 * i for i in range(1, 9)]
        for i in range(len(edges) - 1):
            cols = slice(edges[i], edges[i + 1])
            if i % 3 == 2:
                nc.scalar.activation(out=d[:, cols], in_=d[:, cols], func=ACT.Copy, scale=rinv[:, 0:1])
            else:
                nc.vector.tensor_scalar_mul(out=d[:, cols], in0=d[:, cols], scalar1=rinv[:, 0:1])
            nc.sync.dma_start(out=out[:, cols], in_=d[:, cols])
